import numpy as np
import ml_dtypes


def mxq(x, axis, fmt="e4m3"):
    dtype, down = {"e4m3": (ml_dtypes.float8_e4m3fn, 7), "e5m2": (ml_dtypes.float8_e5m2, 14)}[fmt]
    v = np.moveaxis(np.asarray(x, np.float32).astype(ml_dtypes.bfloat16).astype(np.float64), axis, -1)
    blocks = v.reshape(v.shape[:-1] + (-1, 32))
    amax = np.abs(blocks).max(-1, keepdims=True)
    byte = np.maximum(np.where(amax > 0, np.frexp(amax)[1] - 1 + 127, 0) - down, 1)
    scale = np.exp2(byte - 127.0)
    codes = (blocks / scale).astype(np.float32).astype(dtype).astype(np.float64)
    return np.moveaxis((codes * scale).reshape(v.shape), -1, axis)


WIDE = False


def mx_kscale(k):
    if not WIDE:
        return np.ones(k)
    levels = np.array([10, -10, 5, -5, 0])
    a = np.random.permutation(np.resize(levels, k // 512 * 4)).reshape(k // 512, 4)
    idx = np.arange(k)
    return np.exp2(a[idx // 512, idx % 128 // 32])


BF16 = ml_dtypes.bfloat16


def bf(x):
    return np.asarray(x, np.float32).astype(BF16)


def f64(x):
    return np.asarray(x).astype(np.float64)


B, D, DO, H, T, P = 1024, 1024, 1024, 256, 8, 2


def setup_inputs():
    s = mx_kscale(D)
    return {"transformed": bf(np.random.standard_normal((B, D)) * 1.2 * s),
            "coeff": bf(np.random.standard_normal((B, P)) * 0.45),
            "task_mats": bf(np.random.standard_normal((P, D, D)) / np.sqrt(D) / s[None, :, None] * s[None, None, :])}


def reference(transformed, coeff, task_mats):
    x, c, m = f64(transformed), f64(coeff), f64(task_mats)
    for j in range(P):
        x = x + c[:, j:j + 1] * (mxq(x, 1, "e4m3") @ mxq(m[j], 0, "e4m3"))
    return x

@@ -1,0 +1,264 @@
+from contextlib import ExitStack
+
+import concourse.mybir as mybir
+from concourse.masks import make_identity
+
+F32 = mybir.dt.float32
+BF16 = mybir.dt.bfloat16
+U32 = mybir.dt.uint32
+U8 = mybir.dt.uint8
+FP8X4 = mybir.dt.float8_e4m3fn_x4
+MULT = mybir.AluOpType.mult
+ADD = mybir.AluOpType.add
+
+P = 128
+NB = 8
+D = 1024
+HALF = 512
+FLOPS = 2 * 2 * 1024 * 1024 * 1024
+
+PIN = False
+NV = {(0, 0): 336, (0, 1): 192, (1, 0): 128, (1, 1): 0}
+
+
+def tile_precomputedmetanet_pa_kernel(tc, transformed, coeff, task_mats, out):
+    nc = tc.nc
+    xv = transformed.rearrange("(p m) k -> p m k", m=NB)
+    ov = out.rearrange("(p m) n -> p m n", m=NB)
+    with ExitStack() as ctx:
+        keep = ctx.enter_context(tc.tile_pool(name="keep", bufs=1))
+        stage = ctx.enter_context(tc.tile_pool(name="stage", bufs=2))
+        psum = ctx.enter_context(tc.psum_pool(name="psum", bufs=4))
+        if PIN:
+            ctx.enter_context(tc.manual_schedule())
+
+        ident = keep.tile([P, P], F32, name="ident")
+        make_identity(nc, ident[:])
+        c_bf = keep.tile([P, 2 * NB], BF16, name="c_bf")
+        nc.scalar.dma_start(out=c_bf[:], in_=coeff.rearrange("(p m) j -> p (m j)", m=NB))
+        c32 = keep.tile([P, 2 * NB], F32, name="c32")
+
+        raw = {}
+        xp = {}
+
+        def load_m0(h):
+            raw[(0, h)] = keep.tile([P, 8, HALF], BF16, name="raw0_%d" % h)
+            for g in range(2):
+                for u in range(2):
+                    r0 = 512 * g + 256 * u
+                    nc.sync.dma_start(
+                        out=raw[(0, h)][:, 4 * g + 2 * u : 4 * g + 2 * u + 2, :],
+                        in_=task_mats[0, r0 : r0 + 256, HALF * h : HALF * h + HALF].rearrange(
+                            "(q e) c -> q e c", e=2
+                        ),
+                    )
+
+        def load_m1(h):
+            raw[(1, h)] = keep.tile([P, 8, HALF], BF16, name="raw1_%d" % h)
+            for g in range(2):
+                nc.sync.dma_start(
+                    out=raw[(1, h)][:, 4 * g : 4 * g + 4, :],
+                    in_=task_mats[1, 512 * g : 512 * g + 512, HALF * h : HALF * h + HALF].rearrange(
+                        "(t p) c -> p t c", p=P
+                    ),
+                )
+
+        def load_x(i):
+            xp[i] = keep.tile([P, 2 * D], BF16, name="xp%d" % i)
+            nc.sync.dma_start(
+                out=xp[i][:].rearrange("p (m k) -> p m k", m=2), in_=xv[:, 2 * i : 2 * i + 2, :]
+            )
+
+        load_m0(0)
+        for i in range(4):
+            load_x(i)
+        load_m0(1)
+        load_m1(0)
+        load_m1(1)
+
+        gm = {}
+        cm = {}
+        sm = {}
+
+        def rm(mat, h, g):
+            t = stage.tile([P, 4 * HALF], BF16, name="gm", tag="gm", bufs=4, align_bytes=64)
+            gm[(mat, h, g)] = t
+            dst = t[:].rearrange("p (c i t) -> p c t i", i=4, t=4)
+            src = raw[(mat, h)][:, 4 * g : 4 * g + 4, :].rearrange("p t (c i) -> p c t i", i=4)
+            cv = NV[(mat, h)] // 4
+            if cv > 0:
+                nc.vector.tensor_copy(out=dst[:, 0:cv], in_=src[:, 0:cv])
+            nc.scalar.copy(out=dst[:, cv:], in_=src[:, cv:])
+
+        def qm(mat, h, g):
+            cm[(mat, h, g)] = keep.tile([P, HALF], U32, name="cm%d%d%d" % (mat, h, g), align_bytes=64)
+            sm[(mat, h, g)] = keep.tile([P, HALF], U8, name="sm%d%d%d" % (mat, h, g), align_bytes=64)
+            nc.vector.quantize_mx(
+                out=cm[(mat, h, g)][:].bitcast(FP8X4), scales=sm[(mat, h, g)][:], in_=gm[(mat, h, g)][:]
+            )
+
+        tpx = {}
+        gx = {}
+        cx = {}
+        sx = {}
+
+        def tx(i):
+            xw = xp[i][:].bitcast(F32)
+            for mi in range(2):
+                tp = psum.tile([P, HALF], F32, name="tp", tag="tp")
+                tpx[(i, mi)] = tp
+                for j in range(4):
+                    nc.tensor.transpose(
+                        tp[:, P * j : P * j + P], xw[:, HALF * mi + P * j : HALF * mi + P * j + P], ident[:]
+                    )
+
+        def ex(i):
+            gx[i] = stage.tile([P, 2 * D], BF16, name="gx", tag="gx", bufs=2, align_bytes=64)
+            gw = gx[i][:].bitcast(F32)
+            for mi in range(2):
+                nc.scalar.copy(
+                    out=gw[:, HALF * mi : HALF * mi + HALF].rearrange("p (g b u) -> p g b u", g=2, u=2),
+                    in_=tpx[(i, mi)][:].rearrange("p (g u b) -> p g b u", g=2, u=2),
+                )
+
+        def qx(i):
+            cx[i] = keep.tile([P, HALF], U32, name="cx%d" % i, align_bytes=64)
+            sx[i] = keep.tile([P, HALF], U8, name="sx%d" % i, align_bytes=64)
+            nc.vector.quantize_mx(out=cx[i][:].bitcast(FP8X4), scales=sx[i][:], in_=gx[i][:])
+
+        acc1 = {}
+        x1 = {}
+        tp1 = {}
+        gx1 = {}
+        cx1 = {}
+        sx1 = {}
+        acc2 = {}
+
+        def s1(i, h):
+            for mi in range(2):
+                acc = psum.tile([P, HALF], F32, name="acc", tag="acc")
+                acc1[(i, h, mi)] = acc
+                for g in range(2):
+                    lo = 256 * mi + P * g
+                    nc.tensor.matmul_mx(
+                        out=acc[:],
+                        lhsT=cx[i][:, lo : lo + P].bitcast(FP8X4),
+                        lhsT_scale=sx[i][:, lo : lo + P],
+                        rhs=cm[(0, h, g)][:].bitcast(FP8X4),
+                        rhs_scale=sm[(0, h, g)][:],
+                        start=(g == 0),
+                        stop=(g == 1),
+                    )
+
+        def e1(i, h):
+            for mi in range(2):
+                m = 2 * i + mi
+                x1[(m, h)] = keep.tile([P, HALF], F32, name="x1_%d_%d" % (m, h))
+                nc.vector.scalar_tensor_tensor(
+                    out=x1[(m, h)][:],
+                    in0=acc1[(i, h, mi)][:],
+                    scalar=c32[:, 2 * m : 2 * m + 1],
+                    in1=xp[i][:, D * mi + HALF * h : D * mi + HALF * h + HALF],
+                    op0=MULT,
+                    op1=ADD,
+                )
+
+        def t1(i, h):
+            for mi in range(2):
+                tp = psum.tile([P, HALF], F32, name="tp", tag="tp")
+                tp1[(i, h, mi)] = tp
+                for t in range(4):
+                    nc.tensor.transpose(
+                        tp[:, P * t : P * t + P], x1[(2 * i + mi, h)][:, P * t : P * t + P], ident[:]
+                    )
+
+        def x1x(i, h):
+            gx1[(i, h)] = stage.tile([P, D], BF16, name="gx1", tag="gx1", bufs=4, align_bytes=64)
+            for mi in range(2):
+                nc.scalar.copy(
+                    out=gx1[(i, h)][:, HALF * mi : HALF * mi + HALF].rearrange("p (b t) -> p b t", t=4),
+                    in_=tp1[(i, h, mi)][:].rearrange("p (t b) -> p b t", t=4),
+                )
+
+        def q1(i, h):
+            cx1[(i, h)] = keep.tile([P, 2 * P], U32, name="cx1_%d_%d" % (i, h), align_bytes=64)
+            sx1[(i, h)] = keep.tile([P, 2 * P], U8, name="sx1_%d_%d" % (i, h), align_bytes=64)
+            nc.vector.quantize_mx(
+                out=cx1[(i, h)][:].bitcast(FP8X4), scales=sx1[(i, h)][:], in_=gx1[(i, h)][:]
+            )
+
+        def s2(i, h):
+            for mi in range(2):
+                acc = psum.tile([P, HALF], F32, name="acc", tag="acc")
+                acc2[(i, h, mi)] = acc
+                for g in range(2):
+                    nc.tensor.matmul_mx(
+                        out=acc[:],
+                        lhsT=cx1[(i, g)][:, P * mi : P * mi + P].bitcast(FP8X4),
+                        lhsT_scale=sx1[(i, g)][:, P * mi : P * mi + P],
+                        rhs=cm[(1, h, g)][:].bitcast(FP8X4),
+                        rhs_scale=sm[(1, h, g)][:],
+                        start=(g == 0),
+                        stop=(g == 1),
+                    )
+
+        def e2(i, h):
+            for mi in range(2):
+                m = 2 * i + mi
+                o = stage.tile([P, HALF], F32, name="o", tag="o", bufs=6)
+                nc.vector.scalar_tensor_tensor(
+                    out=o[:],
+                    in0=acc2[(i, h, mi)][:],
+                    scalar=c32[:, 2 * m + 1 : 2 * m + 2],
+                    in1=x1[(m, h)][:],
+                    op0=MULT,
+                    op1=ADD,
+                )
+                nc.sync.dma_start(out=ov[:, m, HALF * h : HALF * h + HALF], in_=o[:])
+
+        extras = {
+            2: [("r", 0, 1, 0), ("r", 0, 1, 1)],
+            3: [("q", 0, 1, 0), ("q", 0, 1, 1)],
+            4: [("r", 1, 0, 0)],
+            5: [("r", 1, 0, 1)],
+            6: [("q", 1, 0, 0), ("q", 1, 0, 1), ("r", 1, 1, 0)],
+            7: [("r", 1, 1, 1)],
+            9: [("q", 1, 1, 0)],
+            10: [("q", 1, 1, 1)],
+        }
+
+        rm(0, 0, 0)
+        rm(0, 0, 1)
+        nc.vector.tensor_copy(out=c32[:], in_=c_bf[:])
+        qm(0, 0, 0)
+        qm(0, 0, 1)
+        tx(0)
+        ex(0)
+        tx(1)
+        ex(1)
+        qx(0)
+        for u in range(16):
+            if u < 8:
+                s1(u % 4, u // 4)
+            else:
+                s2(u % 4, (u - 8) // 4)
+            if u + 2 < 4:
+                tx(u + 2)
+                ex(u + 2)
+            if 1 <= u <= 8:
+                t1((u - 1) % 4, (u - 1) // 4)
+            if u < 8:
+                e1(u % 4, u // 4)
+            else:
+                e2(u % 4, (u - 8) // 4)
+            if u + 1 < 4:
+                qx(u + 1)
+            if 1 <= u <= 8:
+                x1x((u - 1) % 4, (u - 1) // 4)
+            if 2 <= u <= 9:
+                q1((u - 2) % 4, (u - 2) // 4)
+            for kind, mat, h, g in extras.get(u, []):
+                if kind == "r":
+                    rm(mat, h, g)
+                else:
+                    qm(mat, h, g)

@@ -17,7 +17,7 @@ D = 1024
 HALF = 512
 FLOPS = 2 * 2 * 1024 * 1024 * 1024
 
-PIN = False
+PIN = True
 NV = {(0, 0): 336, (0, 1): 192, (1, 0): 128, (1, 1): 0}
 
 

@@ -17,8 +17,43 @@ D = 1024
 HALF = 512
 FLOPS = 2 * 2 * 1024 * 1024 * 1024
 
-PIN = True
-NV = {(0, 0): 336, (0, 1): 192, (1, 0): 128, (1, 1): 0}
+TP_BUFS = 4
+ACC_BUFS = 4
+NV = {(1, 0): 80, (1, 1): 80, (0, 0): 224, (0, 1): 144}
+ORDER = [
+    ("lx", 0), ("lm0", 0, 0), ("lm0", 0, 1), ("lm0", 0, 2), ("lm0", 0, 3), ("lx", 1), ("lm0", 1, 0),
+    ("lm0", 1, 1), ("lm0", 1, 2), ("lm0", 1, 3), ("lx", 2), ("lx", 3), ("lm1", 0, 0), ("lm1", 0, 1),
+    ("lm1", 1, 0), ("lm1", 1, 1), ("tx", 0, 0), ("tx", 0, 1), ("tx", 1, 0), ("tx", 1, 1), ("rm", 0, 0, 0, "V"),
+    ("ex", 0, 0, "S"), ("ex", 0, 1, "S"), ("rm", 0, 0, 0, "S"), ("rm", 0, 0, 1, "S"), ("ex", 1, 0, "S"),
+    ("ex", 1, 1, "S"), ("rm", 0, 1, 0, "S"), ("rm", 0, 1, 1, "S"), ("qx", 0), ("rm", 0, 0, 1, "V"),
+    ("qm", 0, 0, 0), ("qm", 0, 0, 1), ("rm", 0, 1, 0, "V"), ("qx", 1), ("s1", 0, 0, 0), ("s1", 0, 0, 1),
+    ("s1", 1, 0, 0), ("e1", 0, 0, 0), ("e1", 0, 0, 1), ("rm", 0, 1, 1, "V"), ("qm", 0, 1, 0), ("e1", 1, 0, 0),
+    ("qm", 0, 1, 1), ("t1", 0, 0, 0), ("tx", 2, 0), ("tx", 2, 1), ("t1", 0, 0, 1), ("s1", 1, 0, 1),
+    ("s1", 0, 1, 0), ("s1", 0, 1, 1), ("e1", 1, 0, 1), ("ex", 2, 0, "S"), ("ex", 2, 1, "S"),
+    ("x1", 0, 0, 0, "S"), ("x1", 0, 0, 1, "S"), ("rm", 1, 0, 0, "S"), ("tx", 3, 0), ("qx", 2), ("e1", 0, 1, 0),
+    ("q1", 0, 0), ("e1", 0, 1, 1), ("rm", 1, 0, 0, "V"), ("rm", 1, 0, 1, "V"), ("qm", 1, 0, 0),
+    ("rm", 1, 1, 0, "V"), ("t1", 0, 1, 0), ("t1", 0, 1, 1), ("tx", 3, 1), ("s1", 1, 1, 0), ("s1", 1, 1, 1),
+    ("s1", 2, 1, 0), ("e1", 1, 1, 0), ("x1", 0, 1, 0, "S"), ("x1", 0, 1, 1, "S"), ("ex", 3, 0, "S"),
+    ("ex", 3, 1, "S"), ("rm", 1, 0, 1, "S"), ("t1", 1, 1, 0), ("q1", 0, 1), ("e1", 1, 1, 1), ("qx", 3),
+    ("e1", 2, 1, 0), ("rm", 1, 1, 1, "V"), ("x1", 1, 1, 0, "S"), ("t1", 1, 1, 1), ("t1", 1, 0, 0),
+    ("t1", 1, 0, 1), ("s1", 2, 1, 1), ("s1", 2, 0, 0), ("t1", 2, 1, 0), ("e1", 2, 1, 1), ("e1", 2, 0, 0),
+    ("x1", 1, 1, 1, "S"), ("x1", 1, 0, 0, "S"), ("x1", 1, 0, 1, "S"), ("x1", 2, 1, 0, "S"), ("t1", 2, 1, 1),
+    ("t1", 2, 0, 0), ("s1", 2, 0, 1), ("q1", 1, 1), ("qm", 1, 0, 1), ("q1", 1, 0), ("e1", 2, 0, 1),
+    ("x1", 2, 1, 1, "S"), ("x1", 2, 0, 0, "S"), ("rm", 1, 1, 0, "S"), ("s2", 0, 0, 0), ("s2", 0, 0, 1),
+    ("t1", 2, 0, 1), ("s1", 3, 1, 0), ("s1", 3, 1, 1), ("q1", 2, 1), ("e2", 0, 0, 0), ("e2", 0, 0, 1),
+    ("e1", 3, 1, 0), ("e1", 3, 1, 1), ("x1", 2, 0, 1, "S"), ("rm", 1, 1, 1, "S"), ("st", 0, 0, 0),
+    ("st", 0, 0, 1), ("s2", 1, 0, 0), ("t1", 3, 1, 0), ("t1", 3, 1, 1), ("s2", 1, 0, 1), ("s1", 3, 0, 0),
+    ("s1", 3, 0, 1), ("q1", 2, 0), ("e2", 1, 0, 0), ("qm", 1, 1, 0), ("e2", 1, 0, 1), ("e1", 3, 0, 0),
+    ("e1", 3, 0, 1), ("x1", 3, 1, 0, "S"), ("x1", 3, 1, 1, "S"), ("st", 1, 0, 0), ("st", 1, 0, 1),
+    ("s2", 2, 0, 0), ("t1", 3, 0, 0), ("t1", 3, 0, 1), ("s2", 2, 0, 1), ("q1", 3, 1), ("qm", 1, 1, 1),
+    ("e2", 2, 0, 0), ("x1", 3, 0, 0, "S"), ("x1", 3, 0, 1, "S"), ("st", 2, 0, 0), ("s2", 0, 1, 0),
+    ("s2", 0, 1, 1), ("s2", 1, 1, 0), ("q1", 3, 0), ("e2", 2, 0, 1), ("e2", 0, 1, 0), ("e2", 0, 1, 1),
+    ("e2", 1, 1, 0), ("st", 2, 0, 1), ("st", 0, 1, 0), ("st", 0, 1, 1), ("st", 1, 1, 0), ("s2", 1, 1, 1),
+    ("s2", 2, 1, 0), ("s2", 2, 1, 1), ("s2", 3, 1, 0), ("e2", 1, 1, 1), ("e2", 2, 1, 0), ("e2", 2, 1, 1),
+    ("e2", 3, 1, 0), ("st", 1, 1, 1), ("st", 2, 1, 0), ("st", 2, 1, 1), ("st", 3, 1, 0), ("s2", 3, 1, 1),
+    ("s2", 3, 0, 0), ("s2", 3, 0, 1), ("e2", 3, 1, 1), ("e2", 3, 0, 0), ("e2", 3, 0, 1), ("st", 3, 1, 1),
+    ("st", 3, 0, 0), ("st", 3, 0, 1),
+]
 
 
 def tile_precomputedmetanet_pa_kernel(tc, transformed, coeff, task_mats, out):
@@ -27,238 +62,171 @@ def tile_precomputedmetanet_pa_kernel(tc, transformed, coeff, task_mats, out):
     ov = out.rearrange("(p m) n -> p m n", m=NB)
     with ExitStack() as ctx:
         keep = ctx.enter_context(tc.tile_pool(name="keep", bufs=1))
-        stage = ctx.enter_context(tc.tile_pool(name="stage", bufs=2))
-        psum = ctx.enter_context(tc.psum_pool(name="psum", bufs=4))
-        if PIN:
-            ctx.enter_context(tc.manual_schedule())
+        stage = ctx.enter_context(tc.tile_pool(name="stage", bufs=8))
+        psum = ctx.enter_context(tc.psum_pool(name="psum", bufs=1))
+        ctx.enter_context(tc.manual_schedule())
 
         ident = keep.tile([P, P], F32, name="ident")
         make_identity(nc, ident[:])
         c_bf = keep.tile([P, 2 * NB], BF16, name="c_bf")
         nc.scalar.dma_start(out=c_bf[:], in_=coeff.rearrange("(p m) j -> p (m j)", m=NB))
         c32 = keep.tile([P, 2 * NB], F32, name="c32")
+        nc.vector.tensor_copy(out=c32[:], in_=c_bf[:])
 
-        raw = {}
-        xp = {}
+        t = {}
+        count = {"tp": 0, "acc": 0}
 
-        def load_m0(h):
-            raw[(0, h)] = keep.tile([P, 8, HALF], BF16, name="raw0_%d" % h)
-            for g in range(2):
-                for u in range(2):
-                    r0 = 512 * g + 256 * u
-                    nc.sync.dma_start(
-                        out=raw[(0, h)][:, 4 * g + 2 * u : 4 * g + 2 * u + 2, :],
-                        in_=task_mats[0, r0 : r0 + 256, HALF * h : HALF * h + HALF].rearrange(
-                            "(q e) c -> q e c", e=2
-                        ),
-                    )
+        def bank(kind, bufs):
+            k = count[kind]
+            count[kind] = k + 1
+            return psum.tile([P, HALF], F32, name="%s%d" % (kind, k % bufs), tag="%s%d" % (kind, k % bufs))
 
-        def load_m1(h):
-            raw[(1, h)] = keep.tile([P, 8, HALF], BF16, name="raw1_%d" % h)
-            for g in range(2):
-                nc.sync.dma_start(
-                    out=raw[(1, h)][:, 4 * g : 4 * g + 4, :],
-                    in_=task_mats[1, 512 * g : 512 * g + 512, HALF * h : HALF * h + HALF].rearrange(
-                        "(t p) c -> p t c", p=P
-                    ),
-                )
+        def copy_on(eng, dst, src):
+            if eng == "V":
+                nc.vector.tensor_copy(out=dst, in_=src)
+            else:
+                nc.scalar.copy(out=dst, in_=src)
 
-        def load_x(i):
-            xp[i] = keep.tile([P, 2 * D], BF16, name="xp%d" % i)
+        def lx(i):
+            t["xp", i] = keep.tile([P, 2 * D], BF16, name="xp%d" % i)
             nc.sync.dma_start(
-                out=xp[i][:].rearrange("p (m k) -> p m k", m=2), in_=xv[:, 2 * i : 2 * i + 2, :]
+                out=t["xp", i][:].rearrange("p (m k) -> p m k", m=2), in_=xv[:, 2 * i : 2 * i + 2, :]
             )
 
-        load_m0(0)
-        for i in range(4):
-            load_x(i)
-        load_m0(1)
-        load_m1(0)
-        load_m1(1)
+        def lm0(h, k):
+            if k == 0:
+                t["raw", 0, h] = keep.tile([P, 8, HALF], BF16, name="raw0_%d" % h)
+            nc.sync.dma_start(
+                out=t["raw", 0, h][:, 2 * k : 2 * k + 2, :],
+                in_=task_mats[0, 256 * k : 256 * k + 256, HALF * h : HALF * h + HALF].rearrange(
+                    "(q e) c -> q e c", e=2
+                ),
+            )
 
-        gm = {}
-        cm = {}
-        sm = {}
+        def lm1(h, g):
+            if g == 0:
+                t["raw", 1, h] = keep.tile([P, 8, HALF], BF16, name="raw1_%d" % h)
+            nc.sync.dma_start(
+                out=t["raw", 1, h][:, 4 * g : 4 * g + 4, :],
+                in_=task_mats[1, 512 * g : 512 * g + 512, HALF * h : HALF * h + HALF].rearrange(
+                    "(t p) c -> p t c", p=P
+                ),
+            )
 
-        def rm(mat, h, g):
-            t = stage.tile([P, 4 * HALF], BF16, name="gm", tag="gm", bufs=4, align_bytes=64)
-            gm[(mat, h, g)] = t
-            dst = t[:].rearrange("p (c i t) -> p c t i", i=4, t=4)
-            src = raw[(mat, h)][:, 4 * g : 4 * g + 4, :].rearrange("p t (c i) -> p c t i", i=4)
+        def rm(mat, h, g, eng):
+            if ("gm", mat, h, g) not in t:
+                t["gm", mat, h, g] = keep.tile(
+                    [P, 4 * HALF], BF16, name="gm%d%d%d" % (mat, h, g), align_bytes=64
+                )
+            dst = t["gm", mat, h, g][:].rearrange("p (c i t) -> p c t i", i=4, t=4)
+            src = t["raw", mat, h][:, 4 * g : 4 * g + 4, :].rearrange("p t (c i) -> p c t i", i=4)
             cv = NV[(mat, h)] // 4
-            if cv > 0:
+            if eng == "V":
                 nc.vector.tensor_copy(out=dst[:, 0:cv], in_=src[:, 0:cv])
-            nc.scalar.copy(out=dst[:, cv:], in_=src[:, cv:])
+            else:
+                nc.scalar.copy(out=dst[:, cv:], in_=src[:, cv:])
+
+        def quant(key, label, width, src):
+            t[("c",) + key] = keep.tile([P, width], U32, name="c_" + label, align_bytes=64)
+            t[("s",) + key] = keep.tile([P, width], U8, name="s_" + label, align_bytes=64)
+            nc.vector.quantize_mx(out=t[("c",) + key][:].bitcast(FP8X4), scales=t[("s",) + key][:], in_=src)
 
         def qm(mat, h, g):
-            cm[(mat, h, g)] = keep.tile([P, HALF], U32, name="cm%d%d%d" % (mat, h, g), align_bytes=64)
-            sm[(mat, h, g)] = keep.tile([P, HALF], U8, name="sm%d%d%d" % (mat, h, g), align_bytes=64)
-            nc.vector.quantize_mx(
-                out=cm[(mat, h, g)][:].bitcast(FP8X4), scales=sm[(mat, h, g)][:], in_=gm[(mat, h, g)][:]
-            )
+            quant(("m", mat, h, g), "m%d%d%d" % (mat, h, g), HALF, t["gm", mat, h, g][:])
 
-        tpx = {}
-        gx = {}
-        cx = {}
-        sx = {}
-
-        def tx(i):
-            xw = xp[i][:].bitcast(F32)
-            for mi in range(2):
-                tp = psum.tile([P, HALF], F32, name="tp", tag="tp")
-                tpx[(i, mi)] = tp
-                for j in range(4):
-                    nc.tensor.transpose(
-                        tp[:, P * j : P * j + P], xw[:, HALF * mi + P * j : HALF * mi + P * j + P], ident[:]
-                    )
-
-        def ex(i):
-            gx[i] = stage.tile([P, 2 * D], BF16, name="gx", tag="gx", bufs=2, align_bytes=64)
-            gw = gx[i][:].bitcast(F32)
-            for mi in range(2):
-                nc.scalar.copy(
-                    out=gw[:, HALF * mi : HALF * mi + HALF].rearrange("p (g b u) -> p g b u", g=2, u=2),
-                    in_=tpx[(i, mi)][:].rearrange("p (g u b) -> p g b u", g=2, u=2),
+        def tx(i, mi):
+            xw = t["xp", i][:].bitcast(F32)
+            tp = bank("tp", TP_BUFS)
+            t["tpx", i, mi] = tp
+            for j in range(4):
+                nc.tensor.transpose(
+                    tp[:, P * j : P * j + P], xw[:, HALF * mi + P * j : HALF * mi + P * j + P], ident[:]
                 )
+
+        def ex(i, mi, eng):
+            if ("gx", i) not in t:
+                t["gx", i] = keep.tile([P, 2 * D], BF16, name="gx%d" % i, align_bytes=64)
+            gw = t["gx", i][:].bitcast(F32)
+            copy_on(
+                eng,
+                gw[:, HALF * mi : HALF * mi + HALF].rearrange("p (g b u) -> p g b u", g=2, u=2),
+                t["tpx", i, mi][:].rearrange("p (g u b) -> p g b u", g=2, u=2),
+            )
 
         def qx(i):
-            cx[i] = keep.tile([P, HALF], U32, name="cx%d" % i, align_bytes=64)
-            sx[i] = keep.tile([P, HALF], U8, name="sx%d" % i, align_bytes=64)
-            nc.vector.quantize_mx(out=cx[i][:].bitcast(FP8X4), scales=sx[i][:], in_=gx[i][:])
+            quant(("x", i), "x%d" % i, HALF, t["gx", i][:])
 
-        acc1 = {}
-        x1 = {}
-        tp1 = {}
-        gx1 = {}
-        cx1 = {}
-        sx1 = {}
-        acc2 = {}
-
-        def s1(i, h):
-            for mi in range(2):
-                acc = psum.tile([P, HALF], F32, name="acc", tag="acc")
-                acc1[(i, h, mi)] = acc
-                for g in range(2):
-                    lo = 256 * mi + P * g
-                    nc.tensor.matmul_mx(
-                        out=acc[:],
-                        lhsT=cx[i][:, lo : lo + P].bitcast(FP8X4),
-                        lhsT_scale=sx[i][:, lo : lo + P],
-                        rhs=cm[(0, h, g)][:].bitcast(FP8X4),
-                        rhs_scale=sm[(0, h, g)][:],
-                        start=(g == 0),
-                        stop=(g == 1),
-                    )
-
-        def e1(i, h):
-            for mi in range(2):
-                m = 2 * i + mi
-                x1[(m, h)] = keep.tile([P, HALF], F32, name="x1_%d_%d" % (m, h))
-                nc.vector.scalar_tensor_tensor(
-                    out=x1[(m, h)][:],
-                    in0=acc1[(i, h, mi)][:],
-                    scalar=c32[:, 2 * m : 2 * m + 1],
-                    in1=xp[i][:, D * mi + HALF * h : D * mi + HALF * h + HALF],
-                    op0=MULT,
-                    op1=ADD,
+        def mx(acc, ck, lo, mat, h):
+            for g in range(2):
+                key = ck(g)
+                nc.tensor.matmul_mx(
+                    out=acc[:],
+                    lhsT=t[("c",) + key][:, lo(g) : lo(g) + P].bitcast(FP8X4),
+                    lhsT_scale=t[("s",) + key][:, lo(g) : lo(g) + P],
+                    rhs=t["c", "m", mat, h, g][:].bitcast(FP8X4),
+                    rhs_scale=t["s", "m", mat, h, g][:],
+                    start=(g == 0),
+                    stop=(g == 1),
                 )
 
-        def t1(i, h):
-            for mi in range(2):
-                tp = psum.tile([P, HALF], F32, name="tp", tag="tp")
-                tp1[(i, h, mi)] = tp
-                for t in range(4):
-                    nc.tensor.transpose(
-                        tp[:, P * t : P * t + P], x1[(2 * i + mi, h)][:, P * t : P * t + P], ident[:]
-                    )
+        def s1(i, h, mi):
+            t["acc1", i, h, mi] = bank("acc", ACC_BUFS)
+            mx(t["acc1", i, h, mi], lambda g: ("x", i), lambda g: 256 * mi + P * g, 0, h)
 
-        def x1x(i, h):
-            gx1[(i, h)] = stage.tile([P, D], BF16, name="gx1", tag="gx1", bufs=4, align_bytes=64)
-            for mi in range(2):
-                nc.scalar.copy(
-                    out=gx1[(i, h)][:, HALF * mi : HALF * mi + HALF].rearrange("p (b t) -> p b t", t=4),
-                    in_=tp1[(i, h, mi)][:].rearrange("p (t b) -> p b t", t=4),
-                )
-
-        def q1(i, h):
-            cx1[(i, h)] = keep.tile([P, 2 * P], U32, name="cx1_%d_%d" % (i, h), align_bytes=64)
-            sx1[(i, h)] = keep.tile([P, 2 * P], U8, name="sx1_%d_%d" % (i, h), align_bytes=64)
-            nc.vector.quantize_mx(
-                out=cx1[(i, h)][:].bitcast(FP8X4), scales=sx1[(i, h)][:], in_=gx1[(i, h)][:]
+        def e1(i, h, mi):
+            m = 2 * i + mi
+            t["x1", m, h] = keep.tile([P, HALF], F32, name="x1_%d_%d" % (m, h))
+            nc.vector.scalar_tensor_tensor(
+                out=t["x1", m, h][:],
+                in0=t["acc1", i, h, mi][:],
+                scalar=c32[:, 2 * m : 2 * m + 1],
+                in1=t["xp", i][:, D * mi + HALF * h : D * mi + HALF * h + HALF],
+                op0=MULT,
+                op1=ADD,
             )
 
-        def s2(i, h):
-            for mi in range(2):
-                acc = psum.tile([P, HALF], F32, name="acc", tag="acc")
-                acc2[(i, h, mi)] = acc
-                for g in range(2):
-                    nc.tensor.matmul_mx(
-                        out=acc[:],
-                        lhsT=cx1[(i, g)][:, P * mi : P * mi + P].bitcast(FP8X4),
-                        lhsT_scale=sx1[(i, g)][:, P * mi : P * mi + P],
-                        rhs=cm[(1, h, g)][:].bitcast(FP8X4),
-                        rhs_scale=sm[(1, h, g)][:],
-                        start=(g == 0),
-                        stop=(g == 1),
-                    )
-
-        def e2(i, h):
-            for mi in range(2):
-                m = 2 * i + mi
-                o = stage.tile([P, HALF], F32, name="o", tag="o", bufs=6)
-                nc.vector.scalar_tensor_tensor(
-                    out=o[:],
-                    in0=acc2[(i, h, mi)][:],
-                    scalar=c32[:, 2 * m + 1 : 2 * m + 2],
-                    in1=x1[(m, h)][:],
-                    op0=MULT,
-                    op1=ADD,
+        def t1(i, h, mi):
+            tp = bank("tp", TP_BUFS)
+            t["tp1", i, h, mi] = tp
+            for j in range(4):
+                nc.tensor.transpose(
+                    tp[:, P * j : P * j + P], t["x1", 2 * i + mi, h][:, P * j : P * j + P], ident[:]
                 )
-                nc.sync.dma_start(out=ov[:, m, HALF * h : HALF * h + HALF], in_=o[:])
 
-        extras = {
-            2: [("r", 0, 1, 0), ("r", 0, 1, 1)],
-            3: [("q", 0, 1, 0), ("q", 0, 1, 1)],
-            4: [("r", 1, 0, 0)],
-            5: [("r", 1, 0, 1)],
-            6: [("q", 1, 0, 0), ("q", 1, 0, 1), ("r", 1, 1, 0)],
-            7: [("r", 1, 1, 1)],
-            9: [("q", 1, 1, 0)],
-            10: [("q", 1, 1, 1)],
+        def x1(i, h, mi, eng):
+            if ("gx1", i, h) not in t:
+                t["gx1", i, h] = keep.tile([P, D], BF16, name="gx1_%d_%d" % (i, h), align_bytes=64)
+            copy_on(
+                eng,
+                t["gx1", i, h][:, HALF * mi : HALF * mi + HALF].rearrange("p (b j) -> p b j", j=4),
+                t["tp1", i, h, mi][:].rearrange("p (j b) -> p b j", j=4),
+            )
+
+        def q1(i, h):
+            quant(("y", i, h), "y%d%d" % (i, h), 2 * P, t["gx1", i, h][:])
+
+        def s2(i, h, mi):
+            t["acc2", i, h, mi] = bank("acc", ACC_BUFS)
+            mx(t["acc2", i, h, mi], lambda g: ("y", i, g), lambda g: P * mi, 1, h)
+
+        def e2(i, h, mi):
+            m = 2 * i + mi
+            t["o", i, h, mi] = stage.tile([P, HALF], F32, name="o", tag="o")
+            nc.vector.scalar_tensor_tensor(
+                out=t["o", i, h, mi][:],
+                in0=t["acc2", i, h, mi][:],
+                scalar=c32[:, 2 * m + 1 : 2 * m + 2],
+                in1=t["x1", m, h][:],
+                op0=MULT,
+                op1=ADD,
+            )
+
+        def st(i, h, mi):
+            nc.sync.dma_start(out=ov[:, 2 * i + mi, HALF * h : HALF * h + HALF], in_=t["o", i, h, mi][:])
+
+        table = {
+            "lx": lx, "lm0": lm0, "lm1": lm1, "rm": rm, "qm": qm, "tx": tx, "ex": ex, "qx": qx,
+            "s1": s1, "e1": e1, "t1": t1, "x1": x1, "q1": q1, "s2": s2, "e2": e2, "st": st,
         }
-
-        rm(0, 0, 0)
-        rm(0, 0, 1)
-        nc.vector.tensor_copy(out=c32[:], in_=c_bf[:])
-        qm(0, 0, 0)
-        qm(0, 0, 1)
-        tx(0)
-        ex(0)
-        tx(1)
-        ex(1)
-        qx(0)
-        for u in range(16):
-            if u < 8:
-                s1(u % 4, u // 4)
-            else:
-                s2(u % 4, (u - 8) // 4)
-            if u + 2 < 4:
-                tx(u + 2)
-                ex(u + 2)
-            if 1 <= u <= 8:
-                t1((u - 1) % 4, (u - 1) // 4)
-            if u < 8:
-                e1(u % 4, u // 4)
-            else:
-                e2(u % 4, (u - 8) // 4)
-            if u + 1 < 4:
-                qx(u + 1)
-            if 1 <= u <= 8:
-                x1x((u - 1) % 4, (u - 1) // 4)
-            if 2 <= u <= 9:
-                q1((u - 2) % 4, (u - 2) // 4)
-            for kind, mat, h, g in extras.get(u, []):
-                if kind == "r":
-                    rm(mat, h, g)
-                else:
-                    qm(mat, h, g)
+        for step in ORDER:
+            table[step[0]](*step[1:])

@@ -17,43 +17,35 @@ D = 1024
 HALF = 512
 FLOPS = 2 * 2 * 1024 * 1024 * 1024
 
-TP_BUFS = 4
-ACC_BUFS = 4
-NV = {(1, 0): 80, (1, 1): 80, (0, 0): 224, (0, 1): 144}
-ORDER = [
-    ("lx", 0), ("lm0", 0, 0), ("lm0", 0, 1), ("lm0", 0, 2), ("lm0", 0, 3), ("lx", 1), ("lm0", 1, 0),
-    ("lm0", 1, 1), ("lm0", 1, 2), ("lm0", 1, 3), ("lx", 2), ("lx", 3), ("lm1", 0, 0), ("lm1", 0, 1),
-    ("lm1", 1, 0), ("lm1", 1, 1), ("tx", 0, 0), ("tx", 0, 1), ("tx", 1, 0), ("tx", 1, 1), ("rm", 0, 0, 0, "V"),
-    ("ex", 0, 0, "S"), ("ex", 0, 1, "S"), ("rm", 0, 0, 0, "S"), ("rm", 0, 0, 1, "S"), ("ex", 1, 0, "S"),
-    ("ex", 1, 1, "S"), ("rm", 0, 1, 0, "S"), ("rm", 0, 1, 1, "S"), ("qx", 0), ("rm", 0, 0, 1, "V"),
-    ("qm", 0, 0, 0), ("qm", 0, 0, 1), ("rm", 0, 1, 0, "V"), ("qx", 1), ("s1", 0, 0, 0), ("s1", 0, 0, 1),
-    ("s1", 1, 0, 0), ("e1", 0, 0, 0), ("e1", 0, 0, 1), ("rm", 0, 1, 1, "V"), ("qm", 0, 1, 0), ("e1", 1, 0, 0),
-    ("qm", 0, 1, 1), ("t1", 0, 0, 0), ("tx", 2, 0), ("tx", 2, 1), ("t1", 0, 0, 1), ("s1", 1, 0, 1),
-    ("s1", 0, 1, 0), ("s1", 0, 1, 1), ("e1", 1, 0, 1), ("ex", 2, 0, "S"), ("ex", 2, 1, "S"),
-    ("x1", 0, 0, 0, "S"), ("x1", 0, 0, 1, "S"), ("rm", 1, 0, 0, "S"), ("tx", 3, 0), ("qx", 2), ("e1", 0, 1, 0),
-    ("q1", 0, 0), ("e1", 0, 1, 1), ("rm", 1, 0, 0, "V"), ("rm", 1, 0, 1, "V"), ("qm", 1, 0, 0),
-    ("rm", 1, 1, 0, "V"), ("t1", 0, 1, 0), ("t1", 0, 1, 1), ("tx", 3, 1), ("s1", 1, 1, 0), ("s1", 1, 1, 1),
-    ("s1", 2, 1, 0), ("e1", 1, 1, 0), ("x1", 0, 1, 0, "S"), ("x1", 0, 1, 1, "S"), ("ex", 3, 0, "S"),
-    ("ex", 3, 1, "S"), ("rm", 1, 0, 1, "S"), ("t1", 1, 1, 0), ("q1", 0, 1), ("e1", 1, 1, 1), ("qx", 3),
-    ("e1", 2, 1, 0), ("rm", 1, 1, 1, "V"), ("x1", 1, 1, 0, "S"), ("t1", 1, 1, 1), ("t1", 1, 0, 0),
-    ("t1", 1, 0, 1), ("s1", 2, 1, 1), ("s1", 2, 0, 0), ("t1", 2, 1, 0), ("e1", 2, 1, 1), ("e1", 2, 0, 0),
-    ("x1", 1, 1, 1, "S"), ("x1", 1, 0, 0, "S"), ("x1", 1, 0, 1, "S"), ("x1", 2, 1, 0, "S"), ("t1", 2, 1, 1),
-    ("t1", 2, 0, 0), ("s1", 2, 0, 1), ("q1", 1, 1), ("qm", 1, 0, 1), ("q1", 1, 0), ("e1", 2, 0, 1),
-    ("x1", 2, 1, 1, "S"), ("x1", 2, 0, 0, "S"), ("rm", 1, 1, 0, "S"), ("s2", 0, 0, 0), ("s2", 0, 0, 1),
-    ("t1", 2, 0, 1), ("s1", 3, 1, 0), ("s1", 3, 1, 1), ("q1", 2, 1), ("e2", 0, 0, 0), ("e2", 0, 0, 1),
-    ("e1", 3, 1, 0), ("e1", 3, 1, 1), ("x1", 2, 0, 1, "S"), ("rm", 1, 1, 1, "S"), ("st", 0, 0, 0),
-    ("st", 0, 0, 1), ("s2", 1, 0, 0), ("t1", 3, 1, 0), ("t1", 3, 1, 1), ("s2", 1, 0, 1), ("s1", 3, 0, 0),
-    ("s1", 3, 0, 1), ("q1", 2, 0), ("e2", 1, 0, 0), ("qm", 1, 1, 0), ("e2", 1, 0, 1), ("e1", 3, 0, 0),
-    ("e1", 3, 0, 1), ("x1", 3, 1, 0, "S"), ("x1", 3, 1, 1, "S"), ("st", 1, 0, 0), ("st", 1, 0, 1),
-    ("s2", 2, 0, 0), ("t1", 3, 0, 0), ("t1", 3, 0, 1), ("s2", 2, 0, 1), ("q1", 3, 1), ("qm", 1, 1, 1),
-    ("e2", 2, 0, 0), ("x1", 3, 0, 0, "S"), ("x1", 3, 0, 1, "S"), ("st", 2, 0, 0), ("s2", 0, 1, 0),
-    ("s2", 0, 1, 1), ("s2", 1, 1, 0), ("q1", 3, 0), ("e2", 2, 0, 1), ("e2", 0, 1, 0), ("e2", 0, 1, 1),
-    ("e2", 1, 1, 0), ("st", 2, 0, 1), ("st", 0, 1, 0), ("st", 0, 1, 1), ("st", 1, 1, 0), ("s2", 1, 1, 1),
-    ("s2", 2, 1, 0), ("s2", 2, 1, 1), ("s2", 3, 1, 0), ("e2", 1, 1, 1), ("e2", 2, 1, 0), ("e2", 2, 1, 1),
-    ("e2", 3, 1, 0), ("st", 1, 1, 1), ("st", 2, 1, 0), ("st", 2, 1, 1), ("st", 3, 1, 0), ("s2", 3, 1, 1),
-    ("s2", 3, 0, 0), ("s2", 3, 0, 1), ("e2", 3, 1, 1), ("e2", 3, 0, 0), ("e2", 3, 0, 1), ("st", 3, 1, 1),
-    ("st", 3, 0, 0), ("st", 3, 0, 1),
-]
+BANKS = 4
+NV = {(0, 0): 336, (0, 1): 320, (1, 0): 256, (1, 1): 0}
+LOADS = [("x", 0), ("m", 0, 0), ("x", 1), ("m", 0, 1), ("x", 2), ("x", 3), ("m", 1, 0), ("m", 1, 1)]
+GROUPS = [(1, 0, 0), (1, 1, 0), (1, 0, 1), (1, 1, 1), (1, 2, 0), (1, 2, 1), (2, 0, 0), (1, 3, 0), (2, 1, 0), (1, 3, 1), (2, 2, 0), (2, 0, 1), (2, 1, 1), (2, 2, 1), (2, 3, 0), (2, 3, 1)]
+FILL_T = {
+    -1: [0, 1],
+    1: [2],
+    2: [3],
+}
+FILL_S = {
+    -1: [("ex", 0, 0), ("rm", 0, 0, 0), ("ex", 0, 1), ("rm", 0, 0, 1), ("ex", 1, 0), ("rm", 0, 1, 0), ("ex", 1, 1), ("rm", 0, 1, 1)],
+    1: [("ex", 2, 0), ("ex", 2, 1), ("rm", 1, 0, 0)],
+    2: [("rm", 1, 0, 1), ("ex", 3, 0), ("ex", 3, 1)],
+    4: [("rm", 1, 1, 0)],
+    7: [("rm", 1, 1, 1)],
+}
+FILL_V = {
+    -1: [("rm", 0, 0, 0), ("qm", 0, 0, 0), ("rm", 0, 0, 1), ("qx", 0), ("qm", 0, 0, 1), ("rm", 0, 1, 0), ("qm", 0, 1, 0), ("qx", 1), ("rm", 0, 1, 1)],
+    0: [("qm", 0, 1, 1)],
+    1: [("q1", 0, 0)],
+    2: [("rm", 1, 0, 0), ("qx", 2), ("qm", 1, 0, 0)],
+    3: [("rm", 1, 0, 1)],
+    4: [("qx", 3), ("q1", 0, 1), ("qm", 1, 0, 1), ("q1", 1, 0), ("q1", 1, 1)],
+    6: [("qm", 1, 1, 0)],
+    8: [("q1", 2, 0), ("q1", 2, 1)],
+    9: [("qm", 1, 1, 1)],
+    10: [("q1", 3, 0)],
+    12: [("q1", 3, 1)],
+}
 
 
 def tile_precomputedmetanet_pa_kernel(tc, transformed, coeff, task_mats, out):
@@ -76,157 +68,164 @@ def tile_precomputedmetanet_pa_kernel(tc, transformed, coeff, task_mats, out):
         t = {}
         count = {"tp": 0, "acc": 0}
 
-        def bank(kind, bufs):
+        def bank(kind):
             k = count[kind]
             count[kind] = k + 1
-            return psum.tile([P, HALF], F32, name="%s%d" % (kind, k % bufs), tag="%s%d" % (kind, k % bufs))
+            return psum.tile([P, HALF], F32, name="%s%d" % (kind, k % BANKS), tag="%s%d" % (kind, k % BANKS))
 
-        def copy_on(eng, dst, src):
-            if eng == "V":
-                nc.vector.tensor_copy(out=dst, in_=src)
-            else:
-                nc.scalar.copy(out=dst, in_=src)
-
-        def lx(i):
+        def load_x(i):
             t["xp", i] = keep.tile([P, 2 * D], BF16, name="xp%d" % i)
             nc.sync.dma_start(
                 out=t["xp", i][:].rearrange("p (m k) -> p m k", m=2), in_=xv[:, 2 * i : 2 * i + 2, :]
             )
 
-        def lm0(h, k):
-            if k == 0:
-                t["raw", 0, h] = keep.tile([P, 8, HALF], BF16, name="raw0_%d" % h)
-            nc.sync.dma_start(
-                out=t["raw", 0, h][:, 2 * k : 2 * k + 2, :],
-                in_=task_mats[0, 256 * k : 256 * k + 256, HALF * h : HALF * h + HALF].rearrange(
-                    "(q e) c -> q e c", e=2
-                ),
-            )
+        def load_m(mat, h):
+            raw = keep.tile([P, 8, HALF], BF16, name="raw%d_%d" % (mat, h))
+            t["raw", mat, h] = raw
+            cols = slice(HALF * h, HALF * h + HALF)
+            if mat == 0:
+                for k in range(4):
+                    nc.sync.dma_start(
+                        out=raw[:, 2 * k : 2 * k + 2, :],
+                        in_=task_mats[0, 256 * k : 256 * k + 256, cols].rearrange("(q e) c -> q e c", e=2),
+                    )
+            else:
+                for g in range(2):
+                    nc.sync.dma_start(
+                        out=raw[:, 4 * g : 4 * g + 4, :],
+                        in_=task_mats[1, 512 * g : 512 * g + 512, cols].rearrange("(j p) c -> p j c", p=P),
+                    )
 
-        def lm1(h, g):
-            if g == 0:
-                t["raw", 1, h] = keep.tile([P, 8, HALF], BF16, name="raw1_%d" % h)
-            nc.sync.dma_start(
-                out=t["raw", 1, h][:, 4 * g : 4 * g + 4, :],
-                in_=task_mats[1, 512 * g : 512 * g + 512, HALF * h : HALF * h + HALF].rearrange(
-                    "(t p) c -> p t c", p=P
-                ),
-            )
-
-        def rm(mat, h, g, eng):
+        def regroup(on_vector, mat, h, g):
             if ("gm", mat, h, g) not in t:
                 t["gm", mat, h, g] = keep.tile(
                     [P, 4 * HALF], BF16, name="gm%d%d%d" % (mat, h, g), align_bytes=64
                 )
-            dst = t["gm", mat, h, g][:].rearrange("p (c i t) -> p c t i", i=4, t=4)
-            src = t["raw", mat, h][:, 4 * g : 4 * g + 4, :].rearrange("p t (c i) -> p c t i", i=4)
+            dst = t["gm", mat, h, g][:].rearrange("p (c i j) -> p c j i", i=4, j=4)
+            src = t["raw", mat, h][:, 4 * g : 4 * g + 4, :].rearrange("p j (c i) -> p c j i", i=4)
             cv = NV[(mat, h)] // 4
-            if eng == "V":
+            if on_vector:
                 nc.vector.tensor_copy(out=dst[:, 0:cv], in_=src[:, 0:cv])
             else:
                 nc.scalar.copy(out=dst[:, cv:], in_=src[:, cv:])
 
-        def quant(key, label, width, src):
+        def quantise(key, label, width, src):
             t[("c",) + key] = keep.tile([P, width], U32, name="c_" + label, align_bytes=64)
             t[("s",) + key] = keep.tile([P, width], U8, name="s_" + label, align_bytes=64)
             nc.vector.quantize_mx(out=t[("c",) + key][:].bitcast(FP8X4), scales=t[("s",) + key][:], in_=src)
 
-        def qm(mat, h, g):
-            quant(("m", mat, h, g), "m%d%d%d" % (mat, h, g), HALF, t["gm", mat, h, g][:])
-
-        def tx(i, mi):
+        def transpose_x(i):
             xw = t["xp", i][:].bitcast(F32)
-            tp = bank("tp", TP_BUFS)
-            t["tpx", i, mi] = tp
-            for j in range(4):
-                nc.tensor.transpose(
-                    tp[:, P * j : P * j + P], xw[:, HALF * mi + P * j : HALF * mi + P * j + P], ident[:]
-                )
+            for mi in range(2):
+                tp = bank("tp")
+                t["tpx", i, mi] = tp
+                for j in range(4):
+                    nc.tensor.transpose(
+                        tp[:, P * j : P * j + P], xw[:, HALF * mi + P * j : HALF * mi + P * j + P], ident[:]
+                    )
 
-        def ex(i, mi, eng):
+        def copy_x(i, mi):
             if ("gx", i) not in t:
                 t["gx", i] = keep.tile([P, 2 * D], BF16, name="gx%d" % i, align_bytes=64)
             gw = t["gx", i][:].bitcast(F32)
-            copy_on(
-                eng,
-                gw[:, HALF * mi : HALF * mi + HALF].rearrange("p (g b u) -> p g b u", g=2, u=2),
-                t["tpx", i, mi][:].rearrange("p (g u b) -> p g b u", g=2, u=2),
+            nc.scalar.copy(
+                out=gw[:, HALF * mi : HALF * mi + HALF].rearrange("p (g b u) -> p g b u", g=2, u=2),
+                in_=t["tpx", i, mi][:].rearrange("p (g u b) -> p g b u", g=2, u=2),
             )
 
-        def qx(i):
-            quant(("x", i), "x%d" % i, HALF, t["gx", i][:])
+        def passes(stage_no, i, h):
+            for mi in range(2):
+                acc = bank("acc")
+                t["acc", stage_no, i, h, mi] = acc
+                for g in range(2):
+                    if stage_no == 1:
+                        key = ("x", i)
+                        lo = 256 * mi + P * g
+                    else:
+                        key = ("y", i, g)
+                        lo = P * mi
+                    nc.tensor.matmul_mx(
+                        out=acc[:],
+                        lhsT=t[("c",) + key][:, lo : lo + P].bitcast(FP8X4),
+                        lhsT_scale=t[("s",) + key][:, lo : lo + P],
+                        rhs=t["c", "m", stage_no - 1, h, g][:].bitcast(FP8X4),
+                        rhs_scale=t["s", "m", stage_no - 1, h, g][:],
+                        start=(g == 0),
+                        stop=(g == 1),
+                    )
 
-        def mx(acc, ck, lo, mat, h):
-            for g in range(2):
-                key = ck(g)
-                nc.tensor.matmul_mx(
-                    out=acc[:],
-                    lhsT=t[("c",) + key][:, lo(g) : lo(g) + P].bitcast(FP8X4),
-                    lhsT_scale=t[("s",) + key][:, lo(g) : lo(g) + P],
-                    rhs=t["c", "m", mat, h, g][:].bitcast(FP8X4),
-                    rhs_scale=t["s", "m", mat, h, g][:],
-                    start=(g == 0),
-                    stop=(g == 1),
+        def residual(stage_no, i, h):
+            for mi in range(2):
+                m = 2 * i + mi
+                if stage_no == 1:
+                    res = keep.tile([P, HALF], F32, name="x1_%d_%d" % (m, h))
+                    t["x1", m, h] = res
+                    old = t["xp", i][:, D * mi + HALF * h : D * mi + HALF * h + HALF]
+                else:
+                    res = stage.tile([P, HALF], F32, name="o", tag="o")
+                    old = t["x1", m, h][:]
+                nc.vector.scalar_tensor_tensor(
+                    out=res[:],
+                    in0=t["acc", stage_no, i, h, mi][:],
+                    scalar=c32[:, 2 * m + stage_no - 1 : 2 * m + stage_no],
+                    in1=old,
+                    op0=MULT,
+                    op1=ADD,
+                )
+                if stage_no == 2:
+                    nc.sync.dma_start(out=ov[:, m, HALF * h : HALF * h + HALF], in_=res[:])
+
+        def transpose_x1(i, h):
+            for mi in range(2):
+                tp = bank("tp")
+                t["tp1", i, h, mi] = tp
+                for j in range(4):
+                    nc.tensor.transpose(
+                        tp[:, P * j : P * j + P], t["x1", 2 * i + mi, h][:, P * j : P * j + P], ident[:]
+                    )
+
+        def copy_x1(i, h):
+            t["gx1", i, h] = keep.tile([P, D], BF16, name="gx1_%d_%d" % (i, h), align_bytes=64)
+            for mi in range(2):
+                nc.scalar.copy(
+                    out=t["gx1", i, h][:, HALF * mi : HALF * mi + HALF].rearrange("p (b j) -> p b j", j=4),
+                    in_=t["tp1", i, h, mi][:].rearrange("p (j b) -> p b j", j=4),
                 )
 
-        def s1(i, h, mi):
-            t["acc1", i, h, mi] = bank("acc", ACC_BUFS)
-            mx(t["acc1", i, h, mi], lambda g: ("x", i), lambda g: 256 * mi + P * g, 0, h)
+        def fill_scalar(k):
+            for step in FILL_S.get(k, []):
+                if step[0] == "ex":
+                    copy_x(step[1], step[2])
+                else:
+                    regroup(False, step[1], step[2], step[3])
 
-        def e1(i, h, mi):
-            m = 2 * i + mi
-            t["x1", m, h] = keep.tile([P, HALF], F32, name="x1_%d_%d" % (m, h))
-            nc.vector.scalar_tensor_tensor(
-                out=t["x1", m, h][:],
-                in0=t["acc1", i, h, mi][:],
-                scalar=c32[:, 2 * m : 2 * m + 1],
-                in1=t["xp", i][:, D * mi + HALF * h : D * mi + HALF * h + HALF],
-                op0=MULT,
-                op1=ADD,
-            )
+        def fill_vector(k):
+            for step in FILL_V.get(k, []):
+                if step[0] == "rm":
+                    regroup(True, step[1], step[2], step[3])
+                elif step[0] == "qm":
+                    quantise(("m",) + step[1:], "m%d%d%d" % step[1:], HALF, t[("gm",) + step[1:]][:])
+                elif step[0] == "qx":
+                    quantise(("x", step[1]), "x%d" % step[1], HALF, t["gx", step[1]][:])
+                else:
+                    quantise(("y",) + step[1:], "y%d%d" % step[1:], 2 * P, t[("gx1",) + step[1:]][:])
 
-        def t1(i, h, mi):
-            tp = bank("tp", TP_BUFS)
-            t["tp1", i, h, mi] = tp
-            for j in range(4):
-                nc.tensor.transpose(
-                    tp[:, P * j : P * j + P], t["x1", 2 * i + mi, h][:, P * j : P * j + P], ident[:]
-                )
-
-        def x1(i, h, mi, eng):
-            if ("gx1", i, h) not in t:
-                t["gx1", i, h] = keep.tile([P, D], BF16, name="gx1_%d_%d" % (i, h), align_bytes=64)
-            copy_on(
-                eng,
-                t["gx1", i, h][:, HALF * mi : HALF * mi + HALF].rearrange("p (b j) -> p b j", j=4),
-                t["tp1", i, h, mi][:].rearrange("p (j b) -> p b j", j=4),
-            )
-
-        def q1(i, h):
-            quant(("y", i, h), "y%d%d" % (i, h), 2 * P, t["gx1", i, h][:])
-
-        def s2(i, h, mi):
-            t["acc2", i, h, mi] = bank("acc", ACC_BUFS)
-            mx(t["acc2", i, h, mi], lambda g: ("y", i, g), lambda g: P * mi, 1, h)
-
-        def e2(i, h, mi):
-            m = 2 * i + mi
-            t["o", i, h, mi] = stage.tile([P, HALF], F32, name="o", tag="o")
-            nc.vector.scalar_tensor_tensor(
-                out=t["o", i, h, mi][:],
-                in0=t["acc2", i, h, mi][:],
-                scalar=c32[:, 2 * m + 1 : 2 * m + 2],
-                in1=t["x1", m, h][:],
-                op0=MULT,
-                op1=ADD,
-            )
-
-        def st(i, h, mi):
-            nc.sync.dma_start(out=ov[:, 2 * i + mi, HALF * h : HALF * h + HALF], in_=t["o", i, h, mi][:])
-
-        table = {
-            "lx": lx, "lm0": lm0, "lm1": lm1, "rm": rm, "qm": qm, "tx": tx, "ex": ex, "qx": qx,
-            "s1": s1, "e1": e1, "t1": t1, "x1": x1, "q1": q1, "s2": s2, "e2": e2, "st": st,
-        }
-        for step in ORDER:
-            table[step[0]](*step[1:])
+        for item in LOADS:
+            if item[0] == "x":
+                load_x(item[1])
+            else:
+                load_m(item[1], item[2])
+        for k in range(-1, len(GROUPS) + 1):
+            if 0 <= k < len(GROUPS):
+                passes(*GROUPS[k])
+            before = GROUPS[k - 1] if k >= 1 else (0, 0, 0)
+            if before[0] == 1:
+                transpose_x1(before[1], before[2])
+            for i in FILL_T.get(k, []):
+                transpose_x(i)
+            if before[0] == 1:
+                copy_x1(before[1], before[2])
+            fill_scalar(k)
+            if 0 <= k < len(GROUPS):
+                residual(*GROUPS[k])
+            fill_vector(k)

@@ -12,220 +12,216 @@ MULT = mybir.AluOpType.mult
 ADD = mybir.AluOpType.add
 
 P = 128
-NB = 8
+TILES = 8
+PAIRS = TILES // 2
 D = 1024
 HALF = 512
-FLOPS = 2 * 2 * 1024 * 1024 * 1024
+PACK = 4
+FLOPS = 2 * 2 * 1024 * D * D
 
 BANKS = 4
-NV = {(0, 0): 336, (0, 1): 320, (1, 0): 256, (1, 1): 0}
-LOADS = [("x", 0), ("m", 0, 0), ("x", 1), ("m", 0, 1), ("x", 2), ("x", 3), ("m", 1, 0), ("m", 1, 1)]
-GROUPS = [(1, 0, 0), (1, 1, 0), (1, 0, 1), (1, 1, 1), (1, 2, 0), (1, 2, 1), (2, 0, 0), (1, 3, 0), (2, 1, 0), (1, 3, 1), (2, 2, 0), (2, 0, 1), (2, 1, 1), (2, 2, 1), (2, 3, 0), (2, 3, 1)]
-FILL_T = {
-    -1: [0, 1],
-    1: [2],
-    2: [3],
-}
-FILL_S = {
-    -1: [("ex", 0, 0), ("rm", 0, 0, 0), ("ex", 0, 1), ("rm", 0, 0, 1), ("ex", 1, 0), ("rm", 0, 1, 0), ("ex", 1, 1), ("rm", 0, 1, 1)],
-    1: [("ex", 2, 0), ("ex", 2, 1), ("rm", 1, 0, 0)],
-    2: [("rm", 1, 0, 1), ("ex", 3, 0), ("ex", 3, 1)],
-    4: [("rm", 1, 1, 0)],
-    7: [("rm", 1, 1, 1)],
-}
-FILL_V = {
-    -1: [("rm", 0, 0, 0), ("qm", 0, 0, 0), ("rm", 0, 0, 1), ("qx", 0), ("qm", 0, 0, 1), ("rm", 0, 1, 0), ("qm", 0, 1, 0), ("qx", 1), ("rm", 0, 1, 1)],
-    0: [("qm", 0, 1, 1)],
-    1: [("q1", 0, 0)],
-    2: [("rm", 1, 0, 0), ("qx", 2), ("qm", 1, 0, 0)],
-    3: [("rm", 1, 0, 1)],
-    4: [("qx", 3), ("q1", 0, 1), ("qm", 1, 0, 1), ("q1", 1, 0), ("q1", 1, 1)],
-    6: [("qm", 1, 1, 0)],
-    8: [("q1", 2, 0), ("q1", 2, 1)],
-    9: [("qm", 1, 1, 1)],
-    10: [("q1", 3, 0)],
-    12: [("q1", 3, 1)],
-}
+
+X_AHEAD = 3
+REGROUP_AHEAD = 4
+QUANT_AHEAD = 2
+
+VECTOR_COLUMNS = 256
+VECTOR_COLUMNS_LAST = 128
 
 
 def tile_precomputedmetanet_pa_kernel(tc, transformed, coeff, task_mats, out):
     nc = tc.nc
-    xv = transformed.rearrange("(p m) k -> p m k", m=NB)
-    ov = out.rearrange("(p m) n -> p m n", m=NB)
+    x_rows = transformed.rearrange("(p m) k -> p m k", m=TILES)
+    out_rows = out.rearrange("(p m) n -> p m n", m=TILES)
+
+    stage1 = [(1, i, h) for h in range(2) for i in range(2)] + [(1, i, h) for i in range(2, PAIRS) for h in range(2)]
+    stage2 = [(2, i, h) for h in range(2) for i in range(PAIRS - 1)] + [(2, PAIRS - 1, h) for h in range(2)]
+    groups = stage1[:6] + [stage2[0], stage1[6], stage2[1], stage1[7]] + stage2[2:]
+    pair_first = [min(k for k, grp in enumerate(groups) if grp[1] == i) for i in range(PAIRS)]
+    half_first = {
+        (s, h): min(k for k, grp in enumerate(groups) if grp[0] == s and grp[2] == h)
+        for s in (1, 2)
+        for h in range(2)
+    }
+
     with ExitStack() as ctx:
         keep = ctx.enter_context(tc.tile_pool(name="keep", bufs=1))
-        stage = ctx.enter_context(tc.tile_pool(name="stage", bufs=8))
+        results = ctx.enter_context(tc.tile_pool(name="results", bufs=8))
         psum = ctx.enter_context(tc.psum_pool(name="psum", bufs=1))
         ctx.enter_context(tc.manual_schedule())
 
         ident = keep.tile([P, P], F32, name="ident")
         make_identity(nc, ident[:])
-        c_bf = keep.tile([P, 2 * NB], BF16, name="c_bf")
-        nc.scalar.dma_start(out=c_bf[:], in_=coeff.rearrange("(p m) j -> p (m j)", m=NB))
-        c32 = keep.tile([P, 2 * NB], F32, name="c32")
-        nc.vector.tensor_copy(out=c32[:], in_=c_bf[:])
+        coeff_bf = keep.tile([P, 2 * TILES], BF16, name="coeff_bf")
+        nc.scalar.dma_start(out=coeff_bf[:], in_=coeff.rearrange("(p m) j -> p (m j)", m=TILES))
+        coeff_f32 = keep.tile([P, 2 * TILES], F32, name="coeff_f32")
+        nc.vector.tensor_copy(out=coeff_f32[:], in_=coeff_bf[:])
 
-        t = {}
-        count = {"tp": 0, "acc": 0}
+        x_in = {}
+        w_in = {}
+        grouped = {}
+        codes = {}
+        scales = {}
+        banks = {}
+        x1 = {}
+        used = {"t": 0, "s": 0}
 
         def bank(kind):
-            k = count[kind]
-            count[kind] = k + 1
-            return psum.tile([P, HALF], F32, name="%s%d" % (kind, k % BANKS), tag="%s%d" % (kind, k % BANKS))
+            n = used[kind]
+            used[kind] = n + 1
+            return psum.tile([P, HALF], F32, name="%s%d" % (kind, n % BANKS), tag="%s%d" % (kind, n % BANKS))
 
-        def load_x(i):
-            t["xp", i] = keep.tile([P, 2 * D], BF16, name="xp%d" % i)
+        def load_pair(i):
+            x_in[i] = keep.tile([P, 2 * D], BF16, name="x_in%d" % i)
             nc.sync.dma_start(
-                out=t["xp", i][:].rearrange("p (m k) -> p m k", m=2), in_=xv[:, 2 * i : 2 * i + 2, :]
+                out=x_in[i][:].rearrange("p (m k) -> p m k", m=2), in_=x_rows[:, 2 * i : 2 * i + 2, :]
             )
 
-        def load_m(mat, h):
-            raw = keep.tile([P, 8, HALF], BF16, name="raw%d_%d" % (mat, h))
-            t["raw", mat, h] = raw
+        def load_half(s, h):
+            w_in[s, h] = keep.tile([P, 2 * PACK, HALF], BF16, name="w_in%d%d" % (s, h))
             cols = slice(HALF * h, HALF * h + HALF)
-            if mat == 0:
-                for k in range(4):
+            if s == 1:
+                for v in range(4):
                     nc.sync.dma_start(
-                        out=raw[:, 2 * k : 2 * k + 2, :],
-                        in_=task_mats[0, 256 * k : 256 * k + 256, cols].rearrange("(q e) c -> q e c", e=2),
+                        out=w_in[s, h][:, 2 * v : 2 * v + 2, :],
+                        in_=task_mats[0, 256 * v : 256 * v + 256, cols].rearrange("(p e) c -> p e c", e=2),
                     )
             else:
                 for g in range(2):
                     nc.sync.dma_start(
-                        out=raw[:, 4 * g : 4 * g + 4, :],
-                        in_=task_mats[1, 512 * g : 512 * g + 512, cols].rearrange("(j p) c -> p j c", p=P),
+                        out=w_in[s, h][:, PACK * g : PACK * g + PACK, :],
+                        in_=task_mats[1, HALF * g : HALF * g + HALF, cols].rearrange("(j p) c -> p j c", p=P),
                     )
 
-        def regroup(on_vector, mat, h, g):
-            if ("gm", mat, h, g) not in t:
-                t["gm", mat, h, g] = keep.tile(
-                    [P, 4 * HALF], BF16, name="gm%d%d%d" % (mat, h, g), align_bytes=64
+        def regroup(on_vector, s, h, g):
+            if ("w", s, h, g) not in grouped:
+                grouped["w", s, h, g] = keep.tile(
+                    [P, PACK * HALF], BF16, name="grouped_w%d%d%d" % (s, h, g), align_bytes=64
                 )
-            dst = t["gm", mat, h, g][:].rearrange("p (c i j) -> p c j i", i=4, j=4)
-            src = t["raw", mat, h][:, 4 * g : 4 * g + 4, :].rearrange("p j (c i) -> p c j i", i=4)
-            cv = NV[(mat, h)] // 4
+            dst = grouped["w", s, h, g][:].rearrange("p (r i j) -> p r j i", i=4, j=PACK)
+            src = w_in[s, h][:, PACK * g : PACK * g + PACK, :].rearrange("p j (r i) -> p r j i", i=4)
+            runs = (VECTOR_COLUMNS_LAST if (s, h) == (2, 1) else VECTOR_COLUMNS) // 4
             if on_vector:
-                nc.vector.tensor_copy(out=dst[:, 0:cv], in_=src[:, 0:cv])
+                nc.vector.tensor_copy(out=dst[:, :runs], in_=src[:, :runs])
             else:
-                nc.scalar.copy(out=dst[:, cv:], in_=src[:, cv:])
+                nc.scalar.copy(out=dst[:, runs:], in_=src[:, runs:])
 
-        def quantise(key, label, width, src):
-            t[("c",) + key] = keep.tile([P, width], U32, name="c_" + label, align_bytes=64)
-            t[("s",) + key] = keep.tile([P, width], U8, name="s_" + label, align_bytes=64)
-            nc.vector.quantize_mx(out=t[("c",) + key][:].bitcast(FP8X4), scales=t[("s",) + key][:], in_=src)
+        def quantise(key, label, words):
+            codes[key] = keep.tile([P, words], U32, name="codes_" + label, align_bytes=64)
+            scales[key] = keep.tile([P, words], U8, name="scales_" + label, align_bytes=64)
+            nc.vector.quantize_mx(out=codes[key][:].bitcast(FP8X4), scales=scales[key][:], in_=grouped[key][:])
 
-        def transpose_x(i):
-            xw = t["xp", i][:].bitcast(F32)
-            for mi in range(2):
-                tp = bank("tp")
-                t["tpx", i, mi] = tp
-                for j in range(4):
+        def transpose_pair(i):
+            words = x_in[i][:].bitcast(F32)
+            for t in range(2):
+                banks["x", i, t] = bank("t")
+                for v in range(4):
                     nc.tensor.transpose(
-                        tp[:, P * j : P * j + P], xw[:, HALF * mi + P * j : HALF * mi + P * j + P], ident[:]
+                        banks["x", i, t][:, P * v : P * v + P],
+                        words[:, HALF * t + P * v : HALF * t + P * v + P],
+                        ident[:],
                     )
 
-        def copy_x(i, mi):
-            if ("gx", i) not in t:
-                t["gx", i] = keep.tile([P, 2 * D], BF16, name="gx%d" % i, align_bytes=64)
-            gw = t["gx", i][:].bitcast(F32)
-            nc.scalar.copy(
-                out=gw[:, HALF * mi : HALF * mi + HALF].rearrange("p (g b u) -> p g b u", g=2, u=2),
-                in_=t["tpx", i, mi][:].rearrange("p (g u b) -> p g b u", g=2, u=2),
-            )
+        def copy_pair(i):
+            grouped["x", i] = keep.tile([P, 2 * D], BF16, name="grouped_x%d" % i, align_bytes=64)
+            words = grouped["x", i][:].bitcast(F32)
+            for t in range(2):
+                nc.scalar.copy(
+                    out=words[:, HALF * t : HALF * t + HALF].rearrange("p (g b u) -> p g b u", g=2, u=2),
+                    in_=banks["x", i, t][:].rearrange("p (g u b) -> p g b u", g=2, u=2),
+                )
 
-        def passes(stage_no, i, h):
-            for mi in range(2):
-                acc = bank("acc")
-                t["acc", stage_no, i, h, mi] = acc
+        def passes(s, i, h):
+            for t in range(2):
+                banks["sum", s, i, h, t] = bank("s")
                 for g in range(2):
-                    if stage_no == 1:
-                        key = ("x", i)
-                        lo = 256 * mi + P * g
-                    else:
-                        key = ("y", i, g)
-                        lo = P * mi
+                    act = ("x", i) if s == 1 else ("x1", i, g)
+                    lo = P * (2 * t + g) if s == 1 else P * t
                     nc.tensor.matmul_mx(
-                        out=acc[:],
-                        lhsT=t[("c",) + key][:, lo : lo + P].bitcast(FP8X4),
-                        lhsT_scale=t[("s",) + key][:, lo : lo + P],
-                        rhs=t["c", "m", stage_no - 1, h, g][:].bitcast(FP8X4),
-                        rhs_scale=t["s", "m", stage_no - 1, h, g][:],
+                        out=banks["sum", s, i, h, t][:],
+                        lhsT=codes[act][:, lo : lo + P].bitcast(FP8X4),
+                        lhsT_scale=scales[act][:, lo : lo + P],
+                        rhs=codes["w", s, h, g][:].bitcast(FP8X4),
+                        rhs_scale=scales["w", s, h, g][:],
                         start=(g == 0),
                         stop=(g == 1),
                     )
 
-        def residual(stage_no, i, h):
-            for mi in range(2):
-                m = 2 * i + mi
-                if stage_no == 1:
-                    res = keep.tile([P, HALF], F32, name="x1_%d_%d" % (m, h))
-                    t["x1", m, h] = res
-                    old = t["xp", i][:, D * mi + HALF * h : D * mi + HALF * h + HALF]
+        def residual(s, i, h):
+            for t in range(2):
+                m = 2 * i + t
+                if s == 1:
+                    total = keep.tile([P, HALF], F32, name="x1_%d_%d" % (m, h))
+                    x1[m, h] = total
+                    old = x_in[i][:, D * t + HALF * h : D * t + HALF * h + HALF]
                 else:
-                    res = stage.tile([P, HALF], F32, name="o", tag="o")
-                    old = t["x1", m, h][:]
+                    total = results.tile([P, HALF], F32, name="total", tag="total")
+                    old = x1[m, h][:]
                 nc.vector.scalar_tensor_tensor(
-                    out=res[:],
-                    in0=t["acc", stage_no, i, h, mi][:],
-                    scalar=c32[:, 2 * m + stage_no - 1 : 2 * m + stage_no],
+                    out=total[:],
+                    in0=banks["sum", s, i, h, t][:],
+                    scalar=coeff_f32[:, 2 * m + s - 1 : 2 * m + s],
                     in1=old,
                     op0=MULT,
                     op1=ADD,
                 )
-                if stage_no == 2:
-                    nc.sync.dma_start(out=ov[:, m, HALF * h : HALF * h + HALF], in_=res[:])
+                if s == 2:
+                    nc.sync.dma_start(out=out_rows[:, m, HALF * h : HALF * h + HALF], in_=total[:])
 
         def transpose_x1(i, h):
-            for mi in range(2):
-                tp = bank("tp")
-                t["tp1", i, h, mi] = tp
-                for j in range(4):
+            for t in range(2):
+                banks["x1", i, h, t] = bank("t")
+                for j in range(PACK):
                     nc.tensor.transpose(
-                        tp[:, P * j : P * j + P], t["x1", 2 * i + mi, h][:, P * j : P * j + P], ident[:]
+                        banks["x1", i, h, t][:, P * j : P * j + P], x1[2 * i + t, h][:, P * j : P * j + P], ident[:]
                     )
 
         def copy_x1(i, h):
-            t["gx1", i, h] = keep.tile([P, D], BF16, name="gx1_%d_%d" % (i, h), align_bytes=64)
-            for mi in range(2):
+            grouped["x1", i, h] = keep.tile([P, D], BF16, name="grouped_x1_%d%d" % (i, h), align_bytes=64)
+            for t in range(2):
                 nc.scalar.copy(
-                    out=t["gx1", i, h][:, HALF * mi : HALF * mi + HALF].rearrange("p (b j) -> p b j", j=4),
-                    in_=t["tp1", i, h, mi][:].rearrange("p (j b) -> p b j", j=4),
+                    out=grouped["x1", i, h][:, HALF * t : HALF * t + HALF].rearrange("p (b j) -> p b j", j=PACK),
+                    in_=banks["x1", i, h, t][:].rearrange("p (j b) -> p b j", j=PACK),
                 )
 
-        def fill_scalar(k):
-            for step in FILL_S.get(k, []):
-                if step[0] == "ex":
-                    copy_x(step[1], step[2])
-                else:
-                    regroup(False, step[1], step[2], step[3])
-
-        def fill_vector(k):
-            for step in FILL_V.get(k, []):
-                if step[0] == "rm":
-                    regroup(True, step[1], step[2], step[3])
-                elif step[0] == "qm":
-                    quantise(("m",) + step[1:], "m%d%d%d" % step[1:], HALF, t[("gm",) + step[1:]][:])
-                elif step[0] == "qx":
-                    quantise(("x", step[1]), "x%d" % step[1], HALF, t["gx", step[1]][:])
-                else:
-                    quantise(("y",) + step[1:], "y%d%d" % step[1:], 2 * P, t[("gx1",) + step[1:]][:])
-
-        for item in LOADS:
-            if item[0] == "x":
-                load_x(item[1])
+        loads = [(pair_first[i], 0, i) for i in range(PAIRS)] + [(half_first[key], 1, key) for key in half_first]
+        for item in sorted(loads, key=lambda entry: entry[:2]):
+            if item[1] == 0:
+                load_pair(item[2])
             else:
-                load_m(item[1], item[2])
-        for k in range(-1, len(GROUPS) + 1):
-            if 0 <= k < len(GROUPS):
-                passes(*GROUPS[k])
-            before = GROUPS[k - 1] if k >= 1 else (0, 0, 0)
-            if before[0] == 1:
+                load_half(*item[2])
+
+        for k in range(-REGROUP_AHEAD, len(groups)):
+            now = groups[k] if k >= 0 else None
+            before = groups[k - 1] if k >= 1 and groups[k - 1][0] == 1 else None
+            before2 = groups[k - 2] if k >= 2 and groups[k - 2][0] == 1 else None
+            pairs_due = [i for i in range(PAIRS) if pair_first[i] - X_AHEAD == k]
+            chunks_due = [key + (g,) for key in half_first for g in range(2) if half_first[key] - REGROUP_AHEAD + g == k]
+
+            if now:
+                passes(*now)
+            if before:
                 transpose_x1(before[1], before[2])
-            for i in FILL_T.get(k, []):
-                transpose_x(i)
-            if before[0] == 1:
+            for i in pairs_due:
+                transpose_pair(i)
+
+            if before:
                 copy_x1(before[1], before[2])
-            fill_scalar(k)
-            if 0 <= k < len(GROUPS):
-                residual(*GROUPS[k])
-            fill_vector(k)
+            for i in pairs_due:
+                copy_pair(i)
+            for chunk in chunks_due:
+                regroup(False, *chunk)
+
+            if now:
+                residual(*now)
+            for i in range(PAIRS):
+                if pair_first[i] - QUANT_AHEAD == k:
+                    quantise(("x", i), "x%d" % i, HALF)
+            for key in half_first:
+                if half_first[key] - QUANT_AHEAD == k:
+                    for g in range(2):
+                        quantise(("w",) + key + (g,), "w%d%d%d" % (key + (g,)), HALF)
+            if before2:
+                quantise(("x1",) + before2[1:], "x1_%d%d" % before2[1:], 2 * P)
+            for chunk in chunks_due:
+                regroup(True, *chunk)

@@ -21,9 +21,6 @@ FLOPS = 2 * 2 * 1024 * D * D
 
 BANKS = 4
 
-X_AHEAD = 3
-REGROUP_AHEAD = 4
-QUANT_AHEAD = 2
 
 VECTOR_COLUMNS = 256
 VECTOR_COLUMNS_LAST = 128
@@ -37,12 +34,6 @@ def tile_precomputedmetanet_pa_kernel(tc, transformed, coeff, task_mats, out):
     stage1 = [(1, i, h) for h in range(2) for i in range(2)] + [(1, i, h) for i in range(2, PAIRS) for h in range(2)]
     stage2 = [(2, i, h) for h in range(2) for i in range(PAIRS - 1)] + [(2, PAIRS - 1, h) for h in range(2)]
     groups = stage1[:6] + [stage2[0], stage1[6], stage2[1], stage1[7]] + stage2[2:]
-    pair_first = [min(k for k, grp in enumerate(groups) if grp[1] == i) for i in range(PAIRS)]
-    half_first = {
-        (s, h): min(k for k, grp in enumerate(groups) if grp[0] == s and grp[2] == h)
-        for s in (1, 2)
-        for h in range(2)
-    }
 
     with ExitStack() as ctx:
         keep = ctx.enter_context(tc.tile_pool(name="keep", bufs=1))
@@ -78,20 +69,18 @@ def tile_precomputedmetanet_pa_kernel(tc, transformed, coeff, task_mats, out):
             )
 
         def load_half(s, h):
-            w_in[s, h] = keep.tile([P, 2 * PACK, HALF], BF16, name="w_in%d%d" % (s, h))
             cols = slice(HALF * h, HALF * h + HALF)
-            if s == 1:
-                for v in range(4):
-                    nc.sync.dma_start(
-                        out=w_in[s, h][:, 2 * v : 2 * v + 2, :],
-                        in_=task_mats[0, 256 * v : 256 * v + 256, cols].rearrange("(p e) c -> p e c", e=2),
-                    )
-            else:
-                for g in range(2):
-                    nc.sync.dma_start(
-                        out=w_in[s, h][:, PACK * g : PACK * g + PACK, :],
-                        in_=task_mats[1, HALF * g : HALF * g + HALF, cols].rearrange("(j p) c -> p j c", p=P),
-                    )
+            for g in range(2):
+                w_in[s, h, g] = keep.tile([P, PACK, HALF], BF16, name="w_in%d%d%d" % (s, h, g))
+                rows = task_mats[s - 1, HALF * g : HALF * g + HALF, cols]
+                if s == 1:
+                    for u in range(2):
+                        nc.sync.dma_start(
+                            out=w_in[s, h, g][:, 2 * u : 2 * u + 2, :],
+                            in_=rows[256 * u : 256 * u + 256, :].rearrange("(p e) c -> p e c", e=2),
+                        )
+                else:
+                    nc.sync.dma_start(out=w_in[s, h, g][:], in_=rows.rearrange("(j p) c -> p j c", p=P))
 
         def regroup(on_vector, s, h, g):
             if ("w", s, h, g) not in grouped:
@@ -99,7 +88,7 @@ def tile_precomputedmetanet_pa_kernel(tc, transformed, coeff, task_mats, out):
                     [P, PACK * HALF], BF16, name="grouped_w%d%d%d" % (s, h, g), align_bytes=64
                 )
             dst = grouped["w", s, h, g][:].rearrange("p (r i j) -> p r j i", i=4, j=PACK)
-            src = w_in[s, h][:, PACK * g : PACK * g + PACK, :].rearrange("p j (r i) -> p r j i", i=4)
+            src = w_in[s, h, g][:].rearrange("p j (r i) -> p r j i", i=4)
             runs = (VECTOR_COLUMNS_LAST if (s, h) == (2, 1) else VECTOR_COLUMNS) // 4
             if on_vector:
                 nc.vector.tensor_copy(out=dst[:, :runs], in_=src[:, :runs])
@@ -122,14 +111,21 @@ def tile_precomputedmetanet_pa_kernel(tc, transformed, coeff, task_mats, out):
                         ident[:],
                     )
 
-        def copy_pair(i):
-            grouped["x", i] = keep.tile([P, 2 * D], BF16, name="grouped_x%d" % i, align_bytes=64)
-            words = grouped["x", i][:].bitcast(F32)
-            for t in range(2):
-                nc.scalar.copy(
-                    out=words[:, HALF * t : HALF * t + HALF].rearrange("p (g b u) -> p g b u", g=2, u=2),
-                    in_=banks["x", i, t][:].rearrange("p (g u b) -> p g b u", g=2, u=2),
-                )
+        def copy_tile(i, t):
+            if ("x", i) not in grouped:
+                grouped["x", i] = keep.tile([P, 2 * D], BF16, name="grouped_x%d" % i, align_bytes=64)
+            nc.scalar.copy(
+                out=grouped["x", i][:]
+                .bitcast(F32)[:, HALF * t : HALF * t + HALF]
+                .rearrange("p (g b u) -> p g b u", g=2, u=2),
+                in_=banks["x", i, t][:].rearrange("p (g u b) -> p g b u", g=2, u=2),
+            )
+
+        def quantise_pair(i):
+            quantise(("x", i), "x%d" % i, HALF)
+
+        def quantise_chunk(s, c):
+            quantise(("w", s, c // 2, c % 2), "w%d%d" % (s, c), HALF)
 
         def passes(s, i, h):
             for t in range(2):
@@ -184,44 +180,50 @@ def tile_precomputedmetanet_pa_kernel(tc, transformed, coeff, task_mats, out):
                     in_=banks["x1", i, h, t][:].rearrange("p (j b) -> p b j", j=PACK),
                 )
 
-        loads = [(pair_first[i], 0, i) for i in range(PAIRS)] + [(half_first[key], 1, key) for key in half_first]
-        for item in sorted(loads, key=lambda entry: entry[:2]):
-            if item[1] == 0:
-                load_pair(item[2])
-            else:
-                load_half(*item[2])
+        load_pair(0)
+        load_half(1, 0)
+        load_pair(1)
+        load_half(1, 1)
+        load_pair(2)
+        load_pair(3)
+        load_half(2, 0)
+        load_half(2, 1)
 
-        for k in range(-REGROUP_AHEAD, len(groups)):
-            now = groups[k] if k >= 0 else None
+        transpose_pair(0)
+        transpose_pair(1)
+        for r in range(4):
+            copy_tile(r // 2, r % 2)
+            regroup(False, 1, r // 2, r % 2)
+            regroup(True, 1, r // 2, r % 2)
+            if r % 2 == 1:
+                quantise_pair(r // 2)
+            quantise_chunk(1, r)
+
+        for k in range(len(groups)):
             before = groups[k - 1] if k >= 1 and groups[k - 1][0] == 1 else None
             before2 = groups[k - 2] if k >= 2 and groups[k - 2][0] == 1 else None
-            pairs_due = [i for i in range(PAIRS) if pair_first[i] - X_AHEAD == k]
-            chunks_due = [key + (g,) for key in half_first for g in range(2) if half_first[key] - REGROUP_AHEAD + g == k]
+            piece = k // 2
 
-            if now:
-                passes(*now)
+            passes(*groups[k])
             if before:
                 transpose_x1(before[1], before[2])
-            for i in pairs_due:
-                transpose_pair(i)
+            if k % 2 == 0 and piece < 2:
+                transpose_pair(2 + piece)
 
             if before:
                 copy_x1(before[1], before[2])
-            for i in pairs_due:
-                copy_pair(i)
-            for chunk in chunks_due:
-                regroup(False, *chunk)
+            if k % 2 == 0 and piece < 2:
+                copy_tile(2 + piece, 0)
+                copy_tile(2 + piece, 1)
+            if k % 2 == 1 and piece < 4:
+                regroup(False, 2, piece // 2, piece % 2)
 
-            if now:
-                residual(*now)
-            for i in range(PAIRS):
-                if pair_first[i] - QUANT_AHEAD == k:
-                    quantise(("x", i), "x%d" % i, HALF)
-            for key in half_first:
-                if half_first[key] - QUANT_AHEAD == k:
-                    for g in range(2):
-                        quantise(("w",) + key + (g,), "w%d%d%d" % (key + (g,)), HALF)
+            residual(*groups[k])
+            if k % 2 == 1 and piece < 2:
+                quantise_pair(2 + piece)
+            if k % 2 == 0 and 1 <= piece <= 4:
+                quantise_chunk(2, piece - 1)
             if before2:
                 quantise(("x1",) + before2[1:], "x1_%d%d" % before2[1:], 2 * P)
-            for chunk in chunks_due:
-                regroup(True, *chunk)
+            if k % 2 == 1 and piece < 4:
+                regroup(True, 2, piece // 2, piece % 2)

@@ -39,7 +39,6 @@ def tile_precomputedmetanet_pa_kernel(tc, transformed, coeff, task_mats, out):
         keep = ctx.enter_context(tc.tile_pool(name="keep", bufs=1))
         results = ctx.enter_context(tc.tile_pool(name="results", bufs=8))
         psum = ctx.enter_context(tc.psum_pool(name="psum", bufs=1))
-        ctx.enter_context(tc.manual_schedule())
 
         ident = keep.tile([P, P], F32, name="ident")
         make_identity(nc, ident[:])

from contextlib import ExitStack

import concourse.mybir as mybir
from concourse.masks import make_identity

F32 = mybir.dt.float32
BF16 = mybir.dt.bfloat16
U32 = mybir.dt.uint32
U8 = mybir.dt.uint8
FP8X4 = mybir.dt.float8_e4m3fn_x4
MULT = mybir.AluOpType.mult
ADD = mybir.AluOpType.add

P = 128
TILES = 8
PAIRS = TILES // 2
D = 1024
HALF = 512
PACK = 4
FLOPS = 2 * 2 * 1024 * D * D

BANKS = 4


VECTOR_COLUMNS = 256
VECTOR_COLUMNS_LAST = 128


def tile_precomputedmetanet_pa_kernel(tc, transformed, coeff, task_mats, out):
    nc = tc.nc
    x_rows = transformed.rearrange("(p m) k -> p m k", m=TILES)
    out_rows = out.rearrange("(p m) n -> p m n", m=TILES)

    stage1 = [(1, i, h) for h in range(2) for i in range(2)] + [(1, i, h) for i in range(2, PAIRS) for h in range(2)]
    stage2 = [(2, i, h) for h in range(2) for i in range(PAIRS - 1)] + [(2, PAIRS - 1, h) for h in range(2)]
    groups = stage1[:6] + [stage2[0], stage1[6], stage2[1], stage1[7]] + stage2[2:]

    with ExitStack() as ctx:
        keep = ctx.enter_context(tc.tile_pool(name="keep", bufs=1))
        results = ctx.enter_context(tc.tile_pool(name="results", bufs=8))
        psum = ctx.enter_context(tc.psum_pool(name="psum", bufs=1))

        ident = keep.tile([P, P], F32, name="ident")
        make_identity(nc, ident[:])
        coeff_bf = keep.tile([P, 2 * TILES], BF16, name="coeff_bf")
        nc.scalar.dma_start(out=coeff_bf[:], in_=coeff.rearrange("(p m) j -> p (m j)", m=TILES))
        coeff_f32 = keep.tile([P, 2 * TILES], F32, name="coeff_f32")
        nc.vector.tensor_copy(out=coeff_f32[:], in_=coeff_bf[:])

        x_in = {}
        w_in = {}
        grouped = {}
        codes = {}
        scales = {}
        banks = {}
        x1 = {}
        used = {"t": 0, "s": 0}

        def bank(kind):
            n = used[kind]
            used[kind] = n + 1
            return psum.tile([P, HALF], F32, name="%s%d" % (kind, n % BANKS), tag="%s%d" % (kind, n % BANKS))

        def load_pair(i):
            x_in[i] = keep.tile([P, 2 * D], BF16, name="x_in%d" % i)
            nc.sync.dma_start(
                out=x_in[i][:].rearrange("p (m k) -> p m k", m=2), in_=x_rows[:, 2 * i : 2 * i + 2, :]
            )

        def load_half(s, h):
            cols = slice(HALF * h, HALF * h + HALF)
            for g in range(2):
                w_in[s, h, g] = keep.tile([P, PACK, HALF], BF16, name="w_in%d%d%d" % (s, h, g))
                rows = task_mats[s - 1, HALF * g : HALF * g + HALF, cols]
                if s == 1:
                    for u in range(2):
                        nc.sync.dma_start(
                            out=w_in[s, h, g][:, 2 * u : 2 * u + 2, :],
                            in_=rows[256 * u : 256 * u + 256, :].rearrange("(p e) c -> p e c", e=2),
                        )
                else:
                    nc.sync.dma_start(out=w_in[s, h, g][:], in_=rows.rearrange("(j p) c -> p j c", p=P))

        def regroup(on_vector, s, h, g):
            if ("w", s, h, g) not in grouped:
                grouped["w", s, h, g] = keep.tile(
                    [P, PACK * HALF], BF16, name="grouped_w%d%d%d" % (s, h, g), align_bytes=64
                )
            dst = grouped["w", s, h, g][:].rearrange("p (r i j) -> p r j i", i=4, j=PACK)
            src = w_in[s, h, g][:].rearrange("p j (r i) -> p r j i", i=4)
            runs = (VECTOR_COLUMNS_LAST if (s, h) == (2, 1) else VECTOR_COLUMNS) // 4
            if on_vector:
                nc.vector.tensor_copy(out=dst[:, :runs], in_=src[:, :runs])
            else:
                nc.scalar.copy(out=dst[:, runs:], in_=src[:, runs:])

        def quantise(key, label, words):
            codes[key] = keep.tile([P, words], U32, name="codes_" + label, align_bytes=64)
            scales[key] = keep.tile([P, words], U8, name="scales_" + label, align_bytes=64)
            nc.vector.quantize_mx(out=codes[key][:].bitcast(FP8X4), scales=scales[key][:], in_=grouped[key][:])

        def transpose_pair(i):
            words = x_in[i][:].bitcast(F32)
            for t in range(2):
                banks["x", i, t] = bank("t")
                for v in range(4):
                    nc.tensor.transpose(
                        banks["x", i, t][:, P * v : P * v + P],
                        words[:, HALF * t + P * v : HALF * t + P * v + P],
                        ident[:],
                    )

        def copy_tile(i, t):
            if ("x", i) not in grouped:
                grouped["x", i] = keep.tile([P, 2 * D], BF16, name="grouped_x%d" % i, align_bytes=64)
            nc.scalar.copy(
                out=grouped["x", i][:]
                .bitcast(F32)[:, HALF * t : HALF * t + HALF]
                .rearrange("p (g b u) -> p g b u", g=2, u=2),
                in_=banks["x", i, t][:].rearrange("p (g u b) -> p g b u", g=2, u=2),
            )

        def quantise_pair(i):
            quantise(("x", i), "x%d" % i, HALF)

        def quantise_chunk(s, c):
            quantise(("w", s, c // 2, c % 2), "w%d%d" % (s, c), HALF)

        def passes(s, i, h):
            for t in range(2):
                banks["sum", s, i, h, t] = bank("s")
                for g in range(2):
                    act = ("x", i) if s == 1 else ("x1", i, g)
                    lo = P * (2 * t + g) if s == 1 else P * t
                    nc.tensor.matmul_mx(
                        out=banks["sum", s, i, h, t][:],
                        lhsT=codes[act][:, lo : lo + P].bitcast(FP8X4),
                        lhsT_scale=scales[act][:, lo : lo + P],
                        rhs=codes["w", s, h, g][:].bitcast(FP8X4),
                        rhs_scale=scales["w", s, h, g][:],
                        start=(g == 0),
                        stop=(g == 1),
                    )

        def residual(s, i, h):
            for t in range(2):
                m = 2 * i + t
                if s == 1:
                    total = keep.tile([P, HALF], F32, name="x1_%d_%d" % (m, h))
                    x1[m, h] = total
                    old = x_in[i][:, D * t + HALF * h : D * t + HALF * h + HALF]
                else:
                    total = results.tile([P, HALF], F32, name="total", tag="total")
                    old = x1[m, h][:]
                nc.vector.scalar_tensor_tensor(
                    out=total[:],
                    in0=banks["sum", s, i, h, t][:],
                    scalar=coeff_f32[:, 2 * m + s - 1 : 2 * m + s],
                    in1=old,
                    op0=MULT,
                    op1=ADD,
                )
                if s == 2:
                    nc.sync.dma_start(out=out_rows[:, m, HALF * h : HALF * h + HALF], in_=total[:])

        def transpose_x1(i, h):
            for t in range(2):
                banks["x1", i, h, t] = bank("t")
                for j in range(PACK):
                    nc.tensor.transpose(
                        banks["x1", i, h, t][:, P * j : P * j + P], x1[2 * i + t, h][:, P * j : P * j + P], ident[:]
                    )

        def copy_x1(i, h):
            grouped["x1", i, h] = keep.tile([P, D], BF16, name="grouped_x1_%d%d" % (i, h), align_bytes=64)
            for t in range(2):
                nc.scalar.copy(
                    out=grouped["x1", i, h][:, HALF * t : HALF * t + HALF].rearrange("p (b j) -> p b j", j=PACK),
                    in_=banks["x1", i, h, t][:].rearrange("p (j b) -> p b j", j=PACK),
                )

        load_pair(0)
        load_half(1, 0)
        load_pair(1)
        load_half(1, 1)
        load_pair(2)
        load_pair(3)
        load_half(2, 0)
        load_half(2, 1)

        transpose_pair(0)
        transpose_pair(1)
        for r in range(4):
            copy_tile(r // 2, r % 2)
            regroup(False, 1, r // 2, r % 2)
            regroup(True, 1, r // 2, r % 2)
            if r % 2 == 1:
                quantise_pair(r // 2)
            quantise_chunk(1, r)

        for k in range(len(groups)):
            before = groups[k - 1] if k >= 1 and groups[k - 1][0] == 1 else None
            before2 = groups[k - 2] if k >= 2 and groups[k - 2][0] == 1 else None
            piece = k // 2

            passes(*groups[k])
            if before:
                transpose_x1(before[1], before[2])
            if k % 2 == 0 and piece < 2:
                transpose_pair(2 + piece)

            if before:
                copy_x1(before[1], before[2])
            if k % 2 == 0 and piece < 2:
                copy_tile(2 + piece, 0)
                copy_tile(2 + piece, 1)
            if k % 2 == 1 and piece < 4:
                regroup(False, 2, piece // 2, piece % 2)

            residual(*groups[k])
            if k % 2 == 1 and piece < 2:
                quantise_pair(2 + piece)
            if k % 2 == 0 and 1 <= piece <= 4:
                quantise_chunk(2, piece - 1)
            if before2:
                quantise(("x1",) + before2[1:], "x1_%d%d" % before2[1:], 2 * P)
            if k % 2 == 1 and piece < 4:
                regroup(True, 2, piece // 2, piece % 2)
